import numpy as np
import ml_dtypes


def mxq(x, axis, fmt="e4m3"):
    dtype, down = {"e4m3": (ml_dtypes.float8_e4m3fn, 7), "e5m2": (ml_dtypes.float8_e5m2, 14)}[fmt]
    v = np.moveaxis(np.asarray(x, np.float32).astype(ml_dtypes.bfloat16).astype(np.float64), axis, -1)
    blocks = v.reshape(v.shape[:-1] + (-1, 32))
    amax = np.abs(blocks).max(-1, keepdims=True)
    byte = np.maximum(np.where(amax > 0, np.frexp(amax)[1] - 1 + 127, 0) - down, 1)
    scale = np.exp2(byte - 127.0)
    codes = (blocks / scale).astype(np.float32).astype(dtype).astype(np.float64)
    return np.moveaxis((codes * scale).reshape(v.shape), -1, axis)


WIDE = False


def mx_kscale(k):
    if not WIDE:
        return np.ones(k)
    levels = np.array([10, -10, 5, -5, 0])
    a = np.random.permutation(np.resize(levels, k // 512 * 4)).reshape(k // 512, 4)
    idx = np.arange(k)
    return np.exp2(a[idx // 512, idx % 128 // 32])


BF16 = ml_dtypes.bfloat16


def bf(x):
    return np.asarray(x, np.float32).astype(BF16)


def f64(x):
    return np.asarray(x).astype(np.float64)


E2M1 = np.array([0.0, 0.5, 1.0, 1.5, 2.0, 3.0, 4.0, 6.0, -0.0, -0.5, -1.0, -1.5, -2.0, -3.0, -4.0, -6.0])


def pack_weight(w, fmt):
    k, n = w.shape
    w = f64(bf(w)).reshape(k // 32, 32, n)
    amax = np.abs(w).max(1)
    if fmt == "e4m3":
        byte = np.frexp(amax)[1] - 1 + 127 - 7
    else:
        mant, ex = np.frexp(amax / 6.0)
        byte = np.where(mant > 0.5, ex, ex - 1) + 127
    byte = np.clip(np.where(amax > 0, byte, 1), 1, 254)
    scaled = (w * np.exp2(127.0 - byte)[:, None, :]).reshape(k, n).astype(np.float32)
    by_word = np.ascontiguousarray(scaled.reshape(k // 512, 128, 4, n).transpose(0, 1, 3, 2))
    if fmt == "e4m3":
        words = by_word.astype(ml_dtypes.float8_e4m3fn).view(np.uint8)
    else:
        c = by_word.astype(ml_dtypes.float4_e2m1fn).view(np.uint8) & 0xF
        words = c[..., 0::2] | (c[..., 1::2] << 4)
    return np.ascontiguousarray(words), np.ascontiguousarray(byte.astype(np.uint8).reshape(k // 512, 16, n))


def unpack_weight(words, scales, fmt):
    g, p, n, _ = words.shape
    if fmt == "e4m3":
        vals = np.ascontiguousarray(words).view(ml_dtypes.float8_e4m3fn).astype(np.float64)
    else:
        nib = np.empty((g, p, n, 4), np.uint8)
        nib[..., 0::2] = words & 0xF
        nib[..., 1::2] = words >> 4
        vals = E2M1[nib]
    vals = vals * np.repeat(np.exp2(scales.astype(np.float64) - 127.0), 8, axis=1)[..., None]
    return vals.transpose(0, 1, 3, 2).reshape(g * 512, n)


W, M, K, N = 4, 2048, 512, 1024


def setup_inputs():
    s = mx_kscale(K)
    x = bf(np.random.standard_normal((W, M, K)) * s)
    stack = (np.random.standard_normal((W, N, K)) / np.sqrt(W * K) / s).swapaxes(1, 2)
    words, scales = pack_weight(stack.reshape(-1, N), "e4m3")
    bias = bf(np.random.standard_normal((W, M, N)) / np.sqrt(W))
    return {"x": x, "weight_words": words, "weight_scales": scales, "bias": bias}


def reference(x, weight_words, weight_scales, bias):
    w, m, _ = x.shape
    xq = mxq(f64(x), 2, "e4m3")
    wq = unpack_weight(weight_words, weight_scales, "e4m3").reshape(W, K, N)
    y = (xq @ wq).sum(0) + f64(bias).sum(0)
    m_per_rank = m // w
    return y.reshape(w, m_per_rank, -1)

@@ -1,0 +1,216 @@
+from contextlib import ExitStack
+
+import concourse.mybir as mybir
+from concourse.masks import make_identity
+
+BF16 = mybir.dt.bfloat16
+F32 = mybir.dt.float32
+I32 = mybir.dt.int32
+U32 = mybir.dt.uint32
+U8 = mybir.dt.uint8
+FP8X4 = mybir.dt.float8_e4m3fn_x4
+ADD = mybir.AluOpType.add
+
+P = 128
+RANKS = 4
+ROWS = 2048
+K_RANK = 512
+COLS = 1024
+HALF = 512
+ROW_TILES = ROWS // P
+CHUNK = 2
+CHUNKS = ROW_TILES // CHUNK
+X_BUFS = 4
+BIAS_BUFS = 4
+
+FLOPS = 2 * ROWS * RANKS * K_RANK * COLS
+
+
+def tile_gemmrstritonpcie_t_e_kernel(tc, x, weight_words, weight_scales, bias, out):
+    nc = tc.nc
+    left = slice(0, HALF)
+    right = slice(HALF, COLS)
+
+    x_rows = x.rearrange("r (p t) k -> p r t k", t=ROW_TILES)
+    bias_rows = bias.rearrange("r (p t) n -> p r t n", t=ROW_TILES)
+    out_rows = out.rearrange("w (q t) n -> (w q) t n", t=ROW_TILES)
+
+    with ExitStack() as ctx:
+        ctx.enter_context(tc.manual_schedule())
+        keep = ctx.enter_context(tc.tile_pool(name="keep", bufs=1))
+        x_pool = ctx.enter_context(tc.tile_pool(name="x", bufs=X_BUFS))
+        bias_pool = ctx.enter_context(tc.tile_pool(name="bias", bufs=BIAS_BUFS))
+        stage = ctx.enter_context(tc.tile_pool(name="stage", bufs=2))
+        mx_pool = ctx.enter_context(tc.tile_pool(name="mx", bufs=3))
+        out_pool = ctx.enter_context(tc.tile_pool(name="out", bufs=4))
+        flip_psum = ctx.enter_context(tc.psum_pool(name="flip", bufs=2))
+        acc_psum = ctx.enter_context(tc.psum_pool(name="acc", bufs=2))
+
+        x_chunk = {}
+        bias_chunk = {}
+        sorted_words = {}
+        grouped = {}
+        x_codes = {}
+        x_scales = {}
+        product = {}
+        bias_sum = {}
+        left_part = {}
+        right_part = {}
+
+        ident_f32 = keep.tile([P, P], F32)
+        make_identity(nc, ident_f32[:])
+        ident_bf16 = keep.tile([P, P], BF16)
+        make_identity(nc, ident_bf16[:])
+
+        w_planes = keep.tile([P, COLS], U8, align_bytes=64)
+        nc.vector.memset(w_planes[:].bitcast(I32), 0)
+        for quadrant in range(4):
+            nc.sync.dma_start(
+                out=w_planes[32 * quadrant : 32 * quadrant + 16, :].bitcast(I32),
+                in_=weight_scales[:, 4 * quadrant : 4 * quadrant + 4, :].bitcast(I32),
+            )
+        w_words = keep.tile([P, RANKS, COLS], U32, align_bytes=64)
+
+        def load_weight():
+            for g in range(RANKS):
+                nc.sync.dma_start(
+                    out=w_words[:, g, :].bitcast(I32),
+                    in_=weight_words[g].rearrange("p n t -> p (n t)").bitcast(I32),
+                )
+
+        def load_x(j):
+            x_chunk[j] = x_pool.tile([P, RANKS, CHUNK, K_RANK], BF16, name="x_chunk")
+            nc.sync.dma_start(out=x_chunk[j][:], in_=x_rows[:, :, j * CHUNK : (j + 1) * CHUNK, :])
+
+        def load_bias(j):
+            for r in range(RANKS):
+                bias_chunk[(r, j)] = bias_pool.tile([P, CHUNK, COLS], BF16, name="bias_rank%d" % r)
+                nc.sync.dma_start(
+                    out=bias_chunk[(r, j)][:], in_=bias_rows[:, r, j * CHUNK : (j + 1) * CHUNK, :]
+                )
+
+        def bias_block(r, t, cols):
+            return bias_chunk[(r, t // CHUNK)][:, t % CHUNK, cols]
+
+        def sort_words(t):
+            words = x_chunk[t // CHUNK][:, :, t % CHUNK, :].bitcast(F32)
+            sorted_words[t] = stage.tile([P, RANKS, 2, P], F32, name="sorted_words")
+            nc.scalar.copy(out=sorted_words[t][:], in_=words.rearrange("p r (j u) -> p r u j", u=2))
+
+        def flip(t):
+            grouped[t] = stage.tile([P, RANKS, P, 4], BF16, name="grouped", align_bytes=64)
+            grouped_words = (
+                grouped[t][:]
+                .rearrange("p r c f -> p (r c f)")
+                .bitcast(F32)
+                .rearrange("p (r c u) -> p r c u", r=RANKS, u=2)
+            )
+            for pair in range(RANKS // 2):
+                flipped = flip_psum.tile([P, 2, 2, P], F32, name="flipped")
+                for a in range(2):
+                    for u in range(2):
+                        nc.tensor.transpose(
+                            flipped[:, a, u, :], sorted_words[t][:, 2 * pair + a, u, :], ident_f32[:]
+                        )
+                nc.scalar.copy(
+                    out=grouped_words[:, 2 * pair : 2 * pair + 2, :, :],
+                    in_=flipped[:].rearrange("p a u c -> p a c u"),
+                )
+
+        def quantise(t):
+            x_codes[t] = mx_pool.tile([P, RANKS * P], U32, name="x_codes", align_bytes=64)
+            x_scales[t] = mx_pool.tile([P, RANKS * P], U8, name="x_scales", align_bytes=64)
+            nc.vector.quantize_mx(
+                out=x_codes[t][:].bitcast(FP8X4),
+                scales=x_scales[t][:],
+                in_=grouped[t][:].rearrange("p r c f -> p (r c f)"),
+            )
+
+        def multiply(t):
+            product[(t, 0)] = acc_psum.tile([P, HALF], F32, name="product_left")
+            product[(t, 1)] = acc_psum.tile([P, HALF], F32, name="product_right")
+            for g in range(RANKS):
+                rows = slice(g * P, (g + 1) * P)
+                for h, cols in enumerate((left, right)):
+                    nc.tensor.matmul_mx(
+                        out=product[(t, h)][:],
+                        lhsT=x_codes[t][:, rows].bitcast(FP8X4),
+                        lhsT_scale=x_scales[t][:, rows],
+                        rhs=w_words[:, g, cols].bitcast(FP8X4),
+                        rhs_scale=w_planes[4 * g : P, cols],
+                        start=(g == 0),
+                        stop=(g == RANKS - 1),
+                    )
+
+        def sum_bias_on_tensor(t):
+            bias_sum[t] = acc_psum.tile([P, HALF], F32, name="bias_sum")
+            for r in range(1, RANKS):
+                nc.tensor.matmul(
+                    out=bias_sum[t][:],
+                    lhsT=ident_bf16[:],
+                    rhs=bias_block(r, t, left),
+                    start=(r == 1),
+                    stop=(r == RANKS - 1),
+                )
+
+        def start_sums(t):
+            right_part[t] = stage.tile([P, HALF], F32, name="right_part")
+            left_part[t] = stage.tile([P, HALF], F32, name="left_part")
+            nc.vector.tensor_tensor(
+                out=right_part[t][:], in0=bias_block(0, t, right), in1=bias_block(1, t, right), op=ADD
+            )
+            nc.vector.tensor_tensor(
+                out=left_part[t][:], in0=product[(t, 0)][:], in1=bias_block(0, t, left), op=ADD
+            )
+            nc.vector.tensor_tensor(
+                out=right_part[t][:], in0=right_part[t][:], in1=bias_block(2, t, right), op=ADD
+            )
+
+        def add_right_product(t):
+            nc.vector.tensor_tensor(
+                out=right_part[t][:], in0=product[(t, 1)][:], in1=right_part[t][:], op=ADD
+            )
+
+        def finish(t):
+            result = out_pool.tile([P, COLS], F32, name="result")
+            nc.vector.tensor_tensor(
+                out=result[:, left], in0=bias_sum[t][:], in1=left_part[t][:], op=ADD
+            )
+            nc.vector.tensor_tensor(
+                out=result[:, right], in0=right_part[t][:], in1=bias_block(3, t, right), op=ADD
+            )
+            nc.sync.dma_start(out=out_rows[:, t, :], in_=result[:])
+
+        def is_tile(t):
+            return 0 <= t < ROW_TILES
+
+        load_x(0)
+        load_weight()
+        load_x(1)
+        load_x(2)
+        load_bias(0)
+        load_x(3)
+        load_bias(1)
+
+        for i in range(-3, ROW_TILES + 1):
+            if is_tile(i + 3):
+                sort_words(i + 3)
+            if is_tile(i - 1):
+                finish(i - 1)
+            if i % CHUNK == 0:
+                if i // CHUNK + X_BUFS + 1 < CHUNKS:
+                    load_x(i // CHUNK + X_BUFS + 1)
+                if i // CHUNK + BIAS_BUFS - 1 < CHUNKS:
+                    load_bias(i // CHUNK + BIAS_BUFS - 1)
+            if is_tile(i):
+                start_sums(i)
+            if is_tile(i + 2):
+                quantise(i + 2)
+            if is_tile(i):
+                add_right_product(i)
+            if is_tile(i + 1):
+                multiply(i + 1)
+            if is_tile(i):
+                sum_bias_on_tensor(i)
+            if is_tile(i + 3):
+                flip(i + 3)

@@ -41,8 +41,8 @@ def tile_gemmrstritonpcie_t_e_kernel(tc, x, weight_words, weight_scales, bias, o
         x_pool = ctx.enter_context(tc.tile_pool(name="x", bufs=X_BUFS))
         bias_pool = ctx.enter_context(tc.tile_pool(name="bias", bufs=BIAS_BUFS))
         stage = ctx.enter_context(tc.tile_pool(name="stage", bufs=2))
-        mx_pool = ctx.enter_context(tc.tile_pool(name="mx", bufs=3))
-        out_pool = ctx.enter_context(tc.tile_pool(name="out", bufs=4))
+        mx_pool = ctx.enter_context(tc.tile_pool(name="mx", bufs=4))
+        out_pool = ctx.enter_context(tc.tile_pool(name="out", bufs=6))
         flip_psum = ctx.enter_context(tc.psum_pool(name="flip", bufs=2))
         acc_psum = ctx.enter_context(tc.psum_pool(name="acc", bufs=2))
 
@@ -56,6 +56,7 @@ def tile_gemmrstritonpcie_t_e_kernel(tc, x, weight_words, weight_scales, bias, o
         bias_sum = {}
         left_part = {}
         right_part = {}
+        result = {}
 
         ident_f32 = keep.tile([P, P], F32)
         make_identity(nc, ident_f32[:])
@@ -153,36 +154,35 @@ def tile_gemmrstritonpcie_t_e_kernel(tc, x, weight_words, weight_scales, bias, o
                     stop=(r == RANKS - 1),
                 )
 
-        def start_sums(t):
-            right_part[t] = stage.tile([P, HALF], F32, name="right_part")
+        def take_products(t):
             left_part[t] = stage.tile([P, HALF], F32, name="left_part")
-            nc.vector.tensor_tensor(
-                out=right_part[t][:], in0=bias_block(0, t, right), in1=bias_block(1, t, right), op=ADD
-            )
+            right_part[t] = stage.tile([P, HALF], F32, name="right_part")
             nc.vector.tensor_tensor(
                 out=left_part[t][:], in0=product[(t, 0)][:], in1=bias_block(0, t, left), op=ADD
             )
             nc.vector.tensor_tensor(
-                out=right_part[t][:], in0=right_part[t][:], in1=bias_block(2, t, right), op=ADD
+                out=right_part[t][:], in0=product[(t, 1)][:], in1=bias_block(0, t, right), op=ADD
             )
 
-        def add_right_product(t):
+        def add_right_bias(t, r):
             nc.vector.tensor_tensor(
-                out=right_part[t][:], in0=product[(t, 1)][:], in1=right_part[t][:], op=ADD
+                out=right_part[t][:], in0=right_part[t][:], in1=bias_block(r, t, right), op=ADD
             )
 
         def finish(t):
-            result = out_pool.tile([P, COLS], F32, name="result")
+            result[t] = out_pool.tile([P, COLS], F32, name="result")
             nc.vector.tensor_tensor(
-                out=result[:, left], in0=bias_sum[t][:], in1=left_part[t][:], op=ADD
+                out=result[t][:, left], in0=bias_sum[t][:], in1=left_part[t][:], op=ADD
             )
             nc.vector.tensor_tensor(
-                out=result[:, right], in0=right_part[t][:], in1=bias_block(3, t, right), op=ADD
+                out=result[t][:, right], in0=right_part[t][:], in1=bias_block(3, t, right), op=ADD
             )
-            nc.sync.dma_start(out=out_rows[:, t, :], in_=result[:])
 
-        def is_tile(t):
-            return 0 <= t < ROW_TILES
+        def store(t):
+            nc.scalar.dma_start(out=out_rows[:, t, :], in_=result[t][:])
+
+        def tiles(j):
+            return [t for t in range(j * CHUNK, (j + 1) * CHUNK) if 0 <= t < ROW_TILES]
 
         load_x(0)
         load_weight()
@@ -192,25 +192,36 @@ def tile_gemmrstritonpcie_t_e_kernel(tc, x, weight_words, weight_scales, bias, o
         load_x(3)
         load_bias(1)
 
-        for i in range(-3, ROW_TILES + 1):
-            if is_tile(i + 3):
-                sort_words(i + 3)
-            if is_tile(i - 1):
-                finish(i - 1)
-            if i % CHUNK == 0:
-                if i // CHUNK + X_BUFS + 1 < CHUNKS:
-                    load_x(i // CHUNK + X_BUFS + 1)
-                if i // CHUNK + BIAS_BUFS - 1 < CHUNKS:
-                    load_bias(i // CHUNK + BIAS_BUFS - 1)
-            if is_tile(i):
-                start_sums(i)
-            if is_tile(i + 2):
-                quantise(i + 2)
-            if is_tile(i):
-                add_right_product(i)
-            if is_tile(i + 1):
-                multiply(i + 1)
-            if is_tile(i):
-                sum_bias_on_tensor(i)
-            if is_tile(i + 3):
-                flip(i + 3)
+        for j in range(-2, CHUNKS):
+            for t in tiles(j + 2):
+                sort_words(t)
+            if j + 2 + X_BUFS < CHUNKS:
+                load_x(j + 2 + X_BUFS)
+
+            for t in tiles(j + 1)[:1]:
+                quantise(t)
+            for t in tiles(j):
+                take_products(t)
+            for t in tiles(j + 1)[1:]:
+                quantise(t)
+
+            for t in tiles(j + 1)[:1]:
+                multiply(t)
+            for t in tiles(j):
+                sum_bias_on_tensor(t)
+            for t in tiles(j + 2)[:1]:
+                flip(t)
+            for t in tiles(j + 1)[1:]:
+                multiply(t)
+            for t in tiles(j + 2)[1:]:
+                flip(t)
+
+            for r in (1, 2):
+                for t in tiles(j):
+                    add_right_bias(t, r)
+            for t in tiles(j):
+                finish(t)
+            for t in tiles(j):
+                store(t)
+            if 0 <= j + BIAS_BUFS < CHUNKS:
+                load_bias(j + BIAS_BUFS)

@@ -57,6 +57,7 @@ def tile_gemmrstritonpcie_t_e_kernel(tc, x, weight_words, weight_scales, bias, o
         left_part = {}
         right_part = {}
         result = {}
+        right_bias = {}
 
         ident_f32 = keep.tile([P, P], F32)
         make_identity(nc, ident_f32[:])
@@ -164,9 +165,15 @@ def tile_gemmrstritonpcie_t_e_kernel(tc, x, weight_words, weight_scales, bias, o
                 out=right_part[t][:], in0=product[(t, 1)][:], in1=bias_block(0, t, right), op=ADD
             )
 
-        def add_right_bias(t, r):
-            nc.vector.tensor_tensor(
-                out=right_part[t][:], in0=right_part[t][:], in1=bias_block(r, t, right), op=ADD
+        def start_right_bias(t):
+            right_bias[t] = stage.tile([P, HALF], F32, name="right_bias")
+            nc.gpsimd.tensor_tensor(
+                out=right_bias[t][:], in0=bias_block(1, t, right), in1=bias_block(2, t, right), op=ADD
+            )
+
+        def end_right_bias(t):
+            nc.gpsimd.tensor_tensor(
+                out=right_bias[t][:], in0=right_bias[t][:], in1=bias_block(3, t, right), op=ADD
             )
 
         def finish(t):
@@ -175,7 +182,7 @@ def tile_gemmrstritonpcie_t_e_kernel(tc, x, weight_words, weight_scales, bias, o
                 out=result[t][:, left], in0=bias_sum[t][:], in1=left_part[t][:], op=ADD
             )
             nc.vector.tensor_tensor(
-                out=result[t][:, right], in0=right_part[t][:], in1=bias_block(3, t, right), op=ADD
+                out=result[t][:, right], in0=right_part[t][:], in1=right_bias[t][:], op=ADD
             )
 
         def store(t):
@@ -216,9 +223,10 @@ def tile_gemmrstritonpcie_t_e_kernel(tc, x, weight_words, weight_scales, bias, o
             for t in tiles(j + 2)[1:]:
                 flip(t)
 
-            for r in (1, 2):
-                for t in tiles(j):
-                    add_right_bias(t, r)
+            for t in tiles(j):
+                start_right_bias(t)
+            for t in tiles(j):
+                end_right_bias(t)
             for t in tiles(j):
                 finish(t)
             for t in tiles(j):

@@ -21,7 +21,7 @@ ROW_TILES = ROWS // P
 CHUNK = 2
 CHUNKS = ROW_TILES // CHUNK
 X_BUFS = 4
-BIAS_BUFS = 4
+BIAS_BUFS = 8
 
 FLOPS = 2 * ROWS * RANKS * K_RANK * COLS
 
@@ -41,13 +41,14 @@ def tile_gemmrstritonpcie_t_e_kernel(tc, x, weight_words, weight_scales, bias, o
         x_pool = ctx.enter_context(tc.tile_pool(name="x", bufs=X_BUFS))
         bias_pool = ctx.enter_context(tc.tile_pool(name="bias", bufs=BIAS_BUFS))
         stage = ctx.enter_context(tc.tile_pool(name="stage", bufs=2))
+        lone = ctx.enter_context(tc.tile_pool(name="lone", bufs=1))
         mx_pool = ctx.enter_context(tc.tile_pool(name="mx", bufs=4))
         out_pool = ctx.enter_context(tc.tile_pool(name="out", bufs=6))
         flip_psum = ctx.enter_context(tc.psum_pool(name="flip", bufs=2))
         acc_psum = ctx.enter_context(tc.psum_pool(name="acc", bufs=2))
 
         x_chunk = {}
-        bias_chunk = {}
+        bias_tile = {}
         sorted_words = {}
         grouped = {}
         x_codes = {}
@@ -66,12 +67,14 @@ def tile_gemmrstritonpcie_t_e_kernel(tc, x, weight_words, weight_scales, bias, o
 
         w_planes = keep.tile([P, COLS], U8, align_bytes=64)
         nc.vector.memset(w_planes[:].bitcast(I32), 0)
-        for quadrant in range(4):
-            nc.sync.dma_start(
-                out=w_planes[32 * quadrant : 32 * quadrant + 16, :].bitcast(I32),
-                in_=weight_scales[:, 4 * quadrant : 4 * quadrant + 4, :].bitcast(I32),
-            )
         w_words = keep.tile([P, RANKS, COLS], U32, align_bytes=64)
+
+        def load_scales():
+            for quadrant in range(4):
+                nc.sync.dma_start(
+                    out=w_planes[32 * quadrant : 32 * quadrant + 16, :].bitcast(I32),
+                    in_=weight_scales[:, 4 * quadrant : 4 * quadrant + 4, :].bitcast(I32),
+                )
 
         def load_weight():
             for g in range(RANKS):
@@ -84,15 +87,12 @@ def tile_gemmrstritonpcie_t_e_kernel(tc, x, weight_words, weight_scales, bias, o
             x_chunk[j] = x_pool.tile([P, RANKS, CHUNK, K_RANK], BF16, name="x_chunk")
             nc.sync.dma_start(out=x_chunk[j][:], in_=x_rows[:, :, j * CHUNK : (j + 1) * CHUNK, :])
 
-        def load_bias(j):
-            for r in range(RANKS):
-                bias_chunk[(r, j)] = bias_pool.tile([P, CHUNK, COLS], BF16, name="bias_rank%d" % r)
-                nc.sync.dma_start(
-                    out=bias_chunk[(r, j)][:], in_=bias_rows[:, r, j * CHUNK : (j + 1) * CHUNK, :]
-                )
+        def load_bias(t):
+            bias_tile[t] = bias_pool.tile([P, RANKS, COLS], BF16, name="bias_tile")
+            nc.sync.dma_start(out=bias_tile[t][:], in_=bias_rows[:, :, t, :])
 
         def bias_block(r, t, cols):
-            return bias_chunk[(r, t // CHUNK)][:, t % CHUNK, cols]
+            return bias_tile[t][:, r, cols]
 
         def sort_words(t):
             words = x_chunk[t // CHUNK][:, :, t % CHUNK, :].bitcast(F32)
@@ -165,13 +165,11 @@ def tile_gemmrstritonpcie_t_e_kernel(tc, x, weight_words, weight_scales, bias, o
                 out=right_part[t][:], in0=product[(t, 1)][:], in1=bias_block(0, t, right), op=ADD
             )
 
-        def start_right_bias(t):
-            right_bias[t] = stage.tile([P, HALF], F32, name="right_bias")
+        def sum_bias_on_gpsimd(t):
+            right_bias[t] = lone.tile([P, HALF], F32, name="right_bias")
             nc.gpsimd.tensor_tensor(
                 out=right_bias[t][:], in0=bias_block(1, t, right), in1=bias_block(2, t, right), op=ADD
             )
-
-        def end_right_bias(t):
             nc.gpsimd.tensor_tensor(
                 out=right_bias[t][:], in0=right_bias[t][:], in1=bias_block(3, t, right), op=ADD
             )
@@ -179,57 +177,52 @@ def tile_gemmrstritonpcie_t_e_kernel(tc, x, weight_words, weight_scales, bias, o
         def finish(t):
             result[t] = out_pool.tile([P, COLS], F32, name="result")
             nc.vector.tensor_tensor(
-                out=result[t][:, left], in0=bias_sum[t][:], in1=left_part[t][:], op=ADD
+                out=result[t][:, right], in0=right_part[t][:], in1=right_bias[t][:], op=ADD
             )
             nc.vector.tensor_tensor(
-                out=result[t][:, right], in0=right_part[t][:], in1=right_bias[t][:], op=ADD
+                out=result[t][:, left], in0=bias_sum[t][:], in1=left_part[t][:], op=ADD
             )
 
         def store(t):
             nc.scalar.dma_start(out=out_rows[:, t, :], in_=result[t][:])
 
-        def tiles(j):
-            return [t for t in range(j * CHUNK, (j + 1) * CHUNK) if 0 <= t < ROW_TILES]
+        def is_tile(t):
+            return 0 <= t < ROW_TILES
 
         load_x(0)
+        load_scales()
         load_weight()
         load_x(1)
-        load_x(2)
         load_bias(0)
-        load_x(3)
+        load_x(2)
         load_bias(1)
+        load_x(3)
+        load_bias(2)
+        load_bias(3)
+        next_bias = 4
 
-        for j in range(-2, CHUNKS):
-            for t in tiles(j + 2):
-                sort_words(t)
-            if j + 2 + X_BUFS < CHUNKS:
-                load_x(j + 2 + X_BUFS)
-
-            for t in tiles(j + 1)[:1]:
-                quantise(t)
-            for t in tiles(j):
+        for t in range(-4, ROW_TILES + 1):
+            if is_tile(t + 3):
+                flip(t + 3)
+            if is_tile(t + 4):
+                sort_words(t + 4)
+                if (t + 4) % CHUNK == CHUNK - 1 and (t + 4) // CHUNK + X_BUFS < CHUNKS:
+                    load_x((t + 4) // CHUNK + X_BUFS)
+                    if next_bias < BIAS_BUFS:
+                        load_bias(next_bias)
+                        load_bias(next_bias + 1)
+                        next_bias += 2
+            if is_tile(t + 2):
+                quantise(t + 2)
+            if is_tile(t - 1):
+                finish(t - 1)
+                store(t - 1)
+            if is_tile(t):
                 take_products(t)
-            for t in tiles(j + 1)[1:]:
-                quantise(t)
-
-            for t in tiles(j + 1)[:1]:
-                multiply(t)
-            for t in tiles(j):
+            if is_tile(t + 1):
+                multiply(t + 1)
+            if is_tile(t):
                 sum_bias_on_tensor(t)
-            for t in tiles(j + 2)[:1]:
-                flip(t)
-            for t in tiles(j + 1)[1:]:
-                multiply(t)
-            for t in tiles(j + 2)[1:]:
-                flip(t)
-
-            for t in tiles(j):
-                start_right_bias(t)
-            for t in tiles(j):
-                end_right_bias(t)
-            for t in tiles(j):
-                finish(t)
-            for t in tiles(j):
-                store(t)
-            if 0 <= j + BIAS_BUFS < CHUNKS:
-                load_bias(j + BIAS_BUFS)
+                sum_bias_on_gpsimd(t)
+                if t + BIAS_BUFS < ROW_TILES:
+                    load_bias(t + BIAS_BUFS)

@@ -43,7 +43,7 @@ def tile_gemmrstritonpcie_t_e_kernel(tc, x, weight_words, weight_scales, bias, o
         stage = ctx.enter_context(tc.tile_pool(name="stage", bufs=2))
         lone = ctx.enter_context(tc.tile_pool(name="lone", bufs=1))
         mx_pool = ctx.enter_context(tc.tile_pool(name="mx", bufs=4))
-        out_pool = ctx.enter_context(tc.tile_pool(name="out", bufs=6))
+        out_pool = ctx.enter_context(tc.tile_pool(name="out", bufs=12))
         flip_psum = ctx.enter_context(tc.psum_pool(name="flip", bufs=2))
         acc_psum = ctx.enter_context(tc.psum_pool(name="acc", bufs=2))
 
@@ -184,7 +184,7 @@ def tile_gemmrstritonpcie_t_e_kernel(tc, x, weight_words, weight_scales, bias, o
             )
 
         def store(t):
-            nc.scalar.dma_start(out=out_rows[:, t, :], in_=result[t][:])
+            nc.sync.dma_start(out=out_rows[:, t, :], in_=result[t][:])
 
         def is_tile(t):
             return 0 <= t < ROW_TILES

@@ -59,6 +59,7 @@ def tile_gemmrstritonpcie_t_e_kernel(tc, x, weight_words, weight_scales, bias, o
         right_part = {}
         result = {}
         right_bias = {}
+        bias_sum_right = {}
 
         ident_f32 = keep.tile([P, P], F32)
         make_identity(nc, ident_f32[:])
@@ -155,6 +156,17 @@ def tile_gemmrstritonpcie_t_e_kernel(tc, x, weight_words, weight_scales, bias, o
                     stop=(r == RANKS - 1),
                 )
 
+        def sum_right_bias_on_tensor(t):
+            bias_sum_right[t] = acc_psum.tile([P, HALF], F32, name="bias_sum")
+            for r in range(1, RANKS):
+                nc.tensor.matmul(
+                    out=bias_sum_right[t][:],
+                    lhsT=ident_bf16[:],
+                    rhs=bias_block(r, t, right),
+                    start=(r == 1),
+                    stop=(r == RANKS - 1),
+                )
+
         def take_products(t):
             left_part[t] = stage.tile([P, HALF], F32, name="left_part")
             right_part[t] = stage.tile([P, HALF], F32, name="right_part")
@@ -186,6 +198,17 @@ def tile_gemmrstritonpcie_t_e_kernel(tc, x, weight_words, weight_scales, bias, o
         def store(t):
             nc.sync.dma_start(out=out_rows[:, t, :], in_=result[t][:])
 
+        def finish_and_store_last(t):
+            result[t] = out_pool.tile([P, COLS], F32, name="result")
+            nc.vector.tensor_tensor(
+                out=result[t][:, left], in0=bias_sum[t][:], in1=left_part[t][:], op=ADD
+            )
+            nc.sync.dma_start(out=out_rows[:, t, left], in_=result[t][:, left])
+            nc.vector.tensor_tensor(
+                out=result[t][:, right], in0=bias_sum_right[t][:], in1=right_part[t][:], op=ADD
+            )
+            nc.sync.dma_start(out=out_rows[:, t, right], in_=result[t][:, right])
+
         def is_tile(t):
             return 0 <= t < ROW_TILES
 
@@ -214,7 +237,9 @@ def tile_gemmrstritonpcie_t_e_kernel(tc, x, weight_words, weight_scales, bias, o
                         next_bias += 2
             if is_tile(t + 2):
                 quantise(t + 2)
-            if is_tile(t - 1):
+            if t - 1 == ROW_TILES - 1:
+                finish_and_store_last(t - 1)
+            elif is_tile(t - 1):
                 finish(t - 1)
                 store(t - 1)
             if is_tile(t):
@@ -223,6 +248,9 @@ def tile_gemmrstritonpcie_t_e_kernel(tc, x, weight_words, weight_scales, bias, o
                 multiply(t + 1)
             if is_tile(t):
                 sum_bias_on_tensor(t)
-                sum_bias_on_gpsimd(t)
+                if t == ROW_TILES - 1:
+                    sum_right_bias_on_tensor(t)
+                else:
+                    sum_bias_on_gpsimd(t)
                 if t + BIAS_BUFS < ROW_TILES:
                     load_bias(t + BIAS_BUFS)

@@ -41,7 +41,7 @@ def tile_gemmrstritonpcie_t_e_kernel(tc, x, weight_words, weight_scales, bias, o
         x_pool = ctx.enter_context(tc.tile_pool(name="x", bufs=X_BUFS))
         bias_pool = ctx.enter_context(tc.tile_pool(name="bias", bufs=BIAS_BUFS))
         stage = ctx.enter_context(tc.tile_pool(name="stage", bufs=2))
-        lone = ctx.enter_context(tc.tile_pool(name="lone", bufs=1))
+        ahead = ctx.enter_context(tc.tile_pool(name="ahead", bufs=3))
         mx_pool = ctx.enter_context(tc.tile_pool(name="mx", bufs=4))
         out_pool = ctx.enter_context(tc.tile_pool(name="out", bufs=12))
         flip_psum = ctx.enter_context(tc.psum_pool(name="flip", bufs=2))
@@ -178,7 +178,7 @@ def tile_gemmrstritonpcie_t_e_kernel(tc, x, weight_words, weight_scales, bias, o
             )
 
         def sum_bias_on_gpsimd(t):
-            right_bias[t] = lone.tile([P, HALF], F32, name="right_bias")
+            right_bias[t] = ahead.tile([P, HALF], F32, name="right_bias")
             nc.gpsimd.tensor_tensor(
                 out=right_bias[t][:], in0=bias_block(1, t, right), in1=bias_block(2, t, right), op=ADD
             )

@@ -43,7 +43,7 @@ def tile_gemmrstritonpcie_t_e_kernel(tc, x, weight_words, weight_scales, bias, o
         stage = ctx.enter_context(tc.tile_pool(name="stage", bufs=2))
         ahead = ctx.enter_context(tc.tile_pool(name="ahead", bufs=3))
         mx_pool = ctx.enter_context(tc.tile_pool(name="mx", bufs=4))
-        out_pool = ctx.enter_context(tc.tile_pool(name="out", bufs=12))
+        out_pool = ctx.enter_context(tc.tile_pool(name="out", bufs=6))
         flip_psum = ctx.enter_context(tc.psum_pool(name="flip", bufs=2))
         acc_psum = ctx.enter_context(tc.psum_pool(name="acc", bufs=2))
 
@@ -78,11 +78,10 @@ def tile_gemmrstritonpcie_t_e_kernel(tc, x, weight_words, weight_scales, bias, o
                 )
 
         def load_weight():
-            for g in range(RANKS):
-                nc.sync.dma_start(
-                    out=w_words[:, g, :].bitcast(I32),
-                    in_=weight_words[g].rearrange("p n t -> p (n t)").bitcast(I32),
-                )
+            nc.sync.dma_start(
+                out=w_words[:].bitcast(I32),
+                in_=weight_words.rearrange("g p n t -> p g (n t)").bitcast(I32),
+            )
 
         def load_x(j):
             x_chunk[j] = x_pool.tile([P, RANKS, CHUNK, K_RANK], BF16, name="x_chunk")
@@ -186,28 +185,38 @@ def tile_gemmrstritonpcie_t_e_kernel(tc, x, weight_words, weight_scales, bias, o
                 out=right_bias[t][:], in0=right_bias[t][:], in1=bias_block(3, t, right), op=ADD
             )
 
+        def result_rows(t):
+            if t % CHUNK == 0:
+                result[t // CHUNK] = out_pool.tile([P, CHUNK, COLS], F32, name="result")
+            return result[t // CHUNK][:, t % CHUNK, :]
+
         def finish(t):
-            result[t] = out_pool.tile([P, COLS], F32, name="result")
+            rows = result_rows(t)
             nc.vector.tensor_tensor(
-                out=result[t][:, right], in0=right_part[t][:], in1=right_bias[t][:], op=ADD
+                out=rows[:, right], in0=right_part[t][:], in1=right_bias[t][:], op=ADD
             )
             nc.vector.tensor_tensor(
-                out=result[t][:, left], in0=bias_sum[t][:], in1=left_part[t][:], op=ADD
+                out=rows[:, left], in0=bias_sum[t][:], in1=left_part[t][:], op=ADD
             )
 
         def store(t):
-            nc.sync.dma_start(out=out_rows[:, t, :], in_=result[t][:])
+            if t // CHUNK == CHUNKS - 1:
+                nc.sync.dma_start(out=out_rows[:, t, :], in_=result[t // CHUNK][:, t % CHUNK, :])
+            elif t % CHUNK == CHUNK - 1:
+                nc.sync.dma_start(
+                    out=out_rows[:, t - CHUNK + 1 : t + 1, :], in_=result[t // CHUNK][:]
+                )
 
         def finish_and_store_last(t):
-            result[t] = out_pool.tile([P, COLS], F32, name="result")
+            rows = result_rows(t)
             nc.vector.tensor_tensor(
-                out=result[t][:, left], in0=bias_sum[t][:], in1=left_part[t][:], op=ADD
+                out=rows[:, left], in0=bias_sum[t][:], in1=left_part[t][:], op=ADD
             )
-            nc.sync.dma_start(out=out_rows[:, t, left], in_=result[t][:, left])
+            nc.sync.dma_start(out=out_rows[:, t, left], in_=rows[:, left])
             nc.vector.tensor_tensor(
-                out=result[t][:, right], in0=bias_sum_right[t][:], in1=right_part[t][:], op=ADD
+                out=rows[:, right], in0=bias_sum_right[t][:], in1=right_part[t][:], op=ADD
             )
-            nc.sync.dma_start(out=out_rows[:, t, right], in_=result[t][:, right])
+            nc.sync.dma_start(out=out_rows[:, t, right], in_=rows[:, right])
 
         def is_tile(t):
             return 0 <= t < ROW_TILES

@@ -59,7 +59,6 @@ def tile_gemmrstritonpcie_t_e_kernel(tc, x, weight_words, weight_scales, bias, o
         right_part = {}
         result = {}
         right_bias = {}
-        bias_sum_right = {}
 
         ident_f32 = keep.tile([P, P], F32)
         make_identity(nc, ident_f32[:])
@@ -155,17 +154,6 @@ def tile_gemmrstritonpcie_t_e_kernel(tc, x, weight_words, weight_scales, bias, o
                     stop=(r == RANKS - 1),
                 )
 
-        def sum_right_bias_on_tensor(t):
-            bias_sum_right[t] = acc_psum.tile([P, HALF], F32, name="bias_sum")
-            for r in range(1, RANKS):
-                nc.tensor.matmul(
-                    out=bias_sum_right[t][:],
-                    lhsT=ident_bf16[:],
-                    rhs=bias_block(r, t, right),
-                    start=(r == 1),
-                    stop=(r == RANKS - 1),
-                )
-
         def take_products(t):
             left_part[t] = stage.tile([P, HALF], F32, name="left_part")
             right_part[t] = stage.tile([P, HALF], F32, name="right_part")
@@ -210,13 +198,13 @@ def tile_gemmrstritonpcie_t_e_kernel(tc, x, weight_words, weight_scales, bias, o
         def finish_and_store_last(t):
             rows = result_rows(t)
             nc.vector.tensor_tensor(
+                out=rows[:, right], in0=right_part[t][:], in1=right_bias[t][:], op=ADD
+            )
+            nc.sync.dma_start(out=out_rows[:, t, right], in_=rows[:, right])
+            nc.vector.tensor_tensor(
                 out=rows[:, left], in0=bias_sum[t][:], in1=left_part[t][:], op=ADD
             )
             nc.sync.dma_start(out=out_rows[:, t, left], in_=rows[:, left])
-            nc.vector.tensor_tensor(
-                out=rows[:, right], in0=bias_sum_right[t][:], in1=right_part[t][:], op=ADD
-            )
-            nc.sync.dma_start(out=out_rows[:, t, right], in_=rows[:, right])
 
         def is_tile(t):
             return 0 <= t < ROW_TILES
@@ -244,6 +232,8 @@ def tile_gemmrstritonpcie_t_e_kernel(tc, x, weight_words, weight_scales, bias, o
                         load_bias(next_bias)
                         load_bias(next_bias + 1)
                         next_bias += 2
+            if is_tile(t):
+                take_products(t)
             if is_tile(t + 2):
                 quantise(t + 2)
             if t - 1 == ROW_TILES - 1:
@@ -251,15 +241,10 @@ def tile_gemmrstritonpcie_t_e_kernel(tc, x, weight_words, weight_scales, bias, o
             elif is_tile(t - 1):
                 finish(t - 1)
                 store(t - 1)
-            if is_tile(t):
-                take_products(t)
             if is_tile(t + 1):
                 multiply(t + 1)
             if is_tile(t):
                 sum_bias_on_tensor(t)
-                if t == ROW_TILES - 1:
-                    sum_right_bias_on_tensor(t)
-                else:
-                    sum_bias_on_gpsimd(t)
+                sum_bias_on_gpsimd(t)
                 if t + BIAS_BUFS < ROW_TILES:
                     load_bias(t + BIAS_BUFS)

@@ -22,6 +22,7 @@ CHUNK = 2
 CHUNKS = ROW_TILES // CHUNK
 X_BUFS = 4
 BIAS_BUFS = 8
+BIAS_AHEAD = 8
 
 FLOPS = 2 * ROWS * RANKS * K_RANK * COLS
 
@@ -158,10 +159,10 @@ def tile_gemmrstritonpcie_t_e_kernel(tc, x, weight_words, weight_scales, bias, o
             left_part[t] = stage.tile([P, HALF], F32, name="left_part")
             right_part[t] = stage.tile([P, HALF], F32, name="right_part")
             nc.vector.tensor_tensor(
-                out=left_part[t][:], in0=product[(t, 0)][:], in1=bias_block(0, t, left), op=ADD
+                out=right_part[t][:], in0=product[(t, 1)][:], in1=bias_block(0, t, right), op=ADD
             )
             nc.vector.tensor_tensor(
-                out=right_part[t][:], in0=product[(t, 1)][:], in1=bias_block(0, t, right), op=ADD
+                out=left_part[t][:], in0=product[(t, 0)][:], in1=bias_block(0, t, left), op=ADD
             )
 
         def sum_bias_on_gpsimd(t):
@@ -221,7 +222,25 @@ def tile_gemmrstritonpcie_t_e_kernel(tc, x, weight_words, weight_scales, bias, o
         load_bias(3)
         next_bias = 4
 
-        for t in range(-4, ROW_TILES + 1):
+        def finish_and_store(t):
+            if t == ROW_TILES - 1:
+                finish_and_store_last(t)
+            else:
+                finish(t)
+                store(t)
+
+        for t in range(-4, ROW_TILES):
+            bias_first = t >= BIAS_AHEAD
+            if is_tile(t):
+                take_products(t)
+            if is_tile(t + 2):
+                quantise(t + 2)
+            if is_tile(t - 1) and t <= BIAS_AHEAD:
+                finish_and_store(t - 1)
+            if bias_first:
+                sum_bias_on_tensor(t)
+            if is_tile(t + 1):
+                multiply(t + 1)
             if is_tile(t + 3):
                 flip(t + 3)
             if is_tile(t + 4):
@@ -233,18 +252,10 @@ def tile_gemmrstritonpcie_t_e_kernel(tc, x, weight_words, weight_scales, bias, o
                         load_bias(next_bias + 1)
                         next_bias += 2
             if is_tile(t):
-                take_products(t)
-            if is_tile(t + 2):
-                quantise(t + 2)
-            if t - 1 == ROW_TILES - 1:
-                finish_and_store_last(t - 1)
-            elif is_tile(t - 1):
-                finish(t - 1)
-                store(t - 1)
-            if is_tile(t + 1):
-                multiply(t + 1)
-            if is_tile(t):
-                sum_bias_on_tensor(t)
+                if not bias_first:
+                    sum_bias_on_tensor(t)
                 sum_bias_on_gpsimd(t)
+                if bias_first:
+                    finish_and_store(t)
                 if t + BIAS_BUFS < ROW_TILES:
                     load_bias(t + BIAS_BUFS)

@@ -21,7 +21,8 @@ ROW_TILES = ROWS // P
 CHUNK = 2
 CHUNKS = ROW_TILES // CHUNK
 X_BUFS = 4
-BIAS_BUFS = 8
+SINGLE_BIAS = 4
+BIAS_BUFS = 5
 BIAS_AHEAD = 8
 
 FLOPS = 2 * ROWS * RANKS * K_RANK * COLS
@@ -48,7 +49,7 @@ def tile_gemmrstritonpcie_t_e_kernel(tc, x, weight_words, weight_scales, bias, o
         flip_psum = ctx.enter_context(tc.psum_pool(name="flip", bufs=2))
         acc_psum = ctx.enter_context(tc.psum_pool(name="acc", bufs=2))
 
-        x_chunk = {}
+        x_tile = {}
         bias_tile = {}
         sorted_words = {}
         grouped = {}
@@ -83,19 +84,23 @@ def tile_gemmrstritonpcie_t_e_kernel(tc, x, weight_words, weight_scales, bias, o
                 in_=weight_words.rearrange("g p n t -> p g (n t)").bitcast(I32),
             )
 
-        def load_x(j):
-            x_chunk[j] = x_pool.tile([P, RANKS, CHUNK, K_RANK], BF16, name="x_chunk")
-            nc.sync.dma_start(out=x_chunk[j][:], in_=x_rows[:, :, j * CHUNK : (j + 1) * CHUNK, :])
+        def load_x(first, count):
+            rows = x_pool.tile([P, RANKS, count, K_RANK], BF16, name="x_tiles")
+            nc.sync.dma_start(out=rows[:], in_=x_rows[:, :, first : first + count, :])
+            for i in range(count):
+                x_tile[first + i] = rows[:, :, i, :]
 
-        def load_bias(t):
-            bias_tile[t] = bias_pool.tile([P, RANKS, COLS], BF16, name="bias_tile")
-            nc.sync.dma_start(out=bias_tile[t][:], in_=bias_rows[:, :, t, :])
+        def load_bias(first, count):
+            rows = bias_pool.tile([P, RANKS, count, COLS], BF16, name="bias_tiles")
+            nc.sync.dma_start(out=rows[:], in_=bias_rows[:, :, first : first + count, :])
+            for i in range(count):
+                bias_tile[first + i] = rows[:, :, i, :]
 
         def bias_block(r, t, cols):
             return bias_tile[t][:, r, cols]
 
         def sort_words(t):
-            words = x_chunk[t // CHUNK][:, :, t % CHUNK, :].bitcast(F32)
+            words = x_tile[t].bitcast(F32)
             sorted_words[t] = stage.tile([P, RANKS, 2, P], F32, name="sorted_words")
             nc.scalar.copy(out=sorted_words[t][:], in_=words.rearrange("p r (j u) -> p r u j", u=2))
 
@@ -210,17 +215,17 @@ def tile_gemmrstritonpcie_t_e_kernel(tc, x, weight_words, weight_scales, bias, o
         def is_tile(t):
             return 0 <= t < ROW_TILES
 
-        load_x(0)
+        load_x(0, 2)
         load_scales()
         load_weight()
-        load_x(1)
-        load_bias(0)
-        load_x(2)
-        load_bias(1)
-        load_x(3)
-        load_bias(2)
-        load_bias(3)
-        next_bias = 4
+        load_x(2, 2)
+        load_bias(0, 1)
+        load_x(4, 2)
+        load_bias(1, 1)
+        load_x(6, 2)
+        load_bias(2, 1)
+        load_bias(3, 1)
+        next_bias = SINGLE_BIAS
 
         def finish_and_store(t):
             if t == ROW_TILES - 1:
@@ -245,17 +250,17 @@ def tile_gemmrstritonpcie_t_e_kernel(tc, x, weight_words, weight_scales, bias, o
                 flip(t + 3)
             if is_tile(t + 4):
                 sort_words(t + 4)
-                if (t + 4) % CHUNK == CHUNK - 1 and (t + 4) // CHUNK + X_BUFS < CHUNKS:
-                    load_x((t + 4) // CHUNK + X_BUFS)
-                    if next_bias < BIAS_BUFS:
-                        load_bias(next_bias)
-                        load_bias(next_bias + 1)
-                        next_bias += 2
+                if (t + 4) % CHUNK == CHUNK - 1 and t + 5 + CHUNK * (X_BUFS - 1) < ROW_TILES:
+                    load_x(t + 5 + CHUNK * (X_BUFS - 1), CHUNK)
+                    if t + 4 == 1:
+                        load_bias(next_bias, CHUNK)
+                        next_bias += CHUNK
             if is_tile(t):
                 if not bias_first:
                     sum_bias_on_tensor(t)
                 sum_bias_on_gpsimd(t)
                 if bias_first:
                     finish_and_store(t)
-                if t + BIAS_BUFS < ROW_TILES:
-                    load_bias(t + BIAS_BUFS)
+                if (t < SINGLE_BIAS or t % CHUNK == CHUNK - 1) and next_bias < ROW_TILES:
+                    load_bias(next_bias, CHUNK)
+                    next_bias += CHUNK

@@ -21,9 +21,13 @@ ROW_TILES = ROWS // P
 CHUNK = 2
 CHUNKS = ROW_TILES // CHUNK
 X_BUFS = 4
-SINGLE_BIAS = 4
 BIAS_BUFS = 5
-BIAS_AHEAD = 8
+BIAS_AHEAD = 10
+LOADS = (
+    [("x", 2), ("bias", 1), ("x", 2), ("bias", 1)]
+    + [("bias", 2), ("x", 2)] * 5
+    + [("bias", 2), ("bias", 2)]
+)
 
 FLOPS = 2 * ROWS * RANKS * K_RANK * COLS
 
@@ -215,24 +219,38 @@ def tile_gemmrstritonpcie_t_e_kernel(tc, x, weight_words, weight_scales, bias, o
         def is_tile(t):
             return 0 <= t < ROW_TILES
 
-        load_x(0, 2)
+        to_load = list(LOADS)
+        next_tile = {"x": 0, "bias": 0}
+        issued = {"x": [], "bias": []}
+        done_with = {"x": set(), "bias": set()}
+
+        def load_what_fits():
+            while len(to_load) > 0:
+                what, count = to_load[0]
+                load, bufs = {"x": (load_x, X_BUFS), "bias": (load_bias, BIAS_BUFS)}[what]
+                if len(issued[what]) >= bufs and not issued[what][-bufs] <= done_with[what]:
+                    return
+                first = next_tile[what]
+                load(first, count)
+                issued[what].append(set(range(first, first + count)))
+                next_tile[what] = first + count
+                to_load.remove(to_load[0])
+
+        load_x(0, CHUNK)
+        issued["x"].append(set(range(CHUNK)))
+        next_tile["x"] = CHUNK
         load_scales()
         load_weight()
-        load_x(2, 2)
-        load_bias(0, 1)
-        load_x(4, 2)
-        load_bias(1, 1)
-        load_x(6, 2)
-        load_bias(2, 1)
-        load_bias(3, 1)
-        next_bias = SINGLE_BIAS
+        load_what_fits()
+
+        to_store = []
 
         def finish_and_store(t):
             if t == ROW_TILES - 1:
                 finish_and_store_last(t)
             else:
                 finish(t)
-                store(t)
+                to_store.append(t)
 
         for t in range(-4, ROW_TILES):
             bias_first = t >= BIAS_AHEAD
@@ -250,17 +268,17 @@ def tile_gemmrstritonpcie_t_e_kernel(tc, x, weight_words, weight_scales, bias, o
                 flip(t + 3)
             if is_tile(t + 4):
                 sort_words(t + 4)
-                if (t + 4) % CHUNK == CHUNK - 1 and t + 5 + CHUNK * (X_BUFS - 1) < ROW_TILES:
-                    load_x(t + 5 + CHUNK * (X_BUFS - 1), CHUNK)
-                    if t + 4 == 1:
-                        load_bias(next_bias, CHUNK)
-                        next_bias += CHUNK
+                done_with["x"].add(t + 4)
+                load_what_fits()
             if is_tile(t):
                 if not bias_first:
                     sum_bias_on_tensor(t)
                 sum_bias_on_gpsimd(t)
                 if bias_first:
                     finish_and_store(t)
-                if (t < SINGLE_BIAS or t % CHUNK == CHUNK - 1) and next_bias < ROW_TILES:
-                    load_bias(next_bias, CHUNK)
-                    next_bias += CHUNK
+                done_with["bias"].add(t)
+                load_what_fits()
+            if len(to_load) == 0:
+                for finished in to_store:
+                    store(finished)
+                to_store.clear()

@@ -20,13 +20,13 @@ HALF = 512
 ROW_TILES = ROWS // P
 CHUNK = 2
 CHUNKS = ROW_TILES // CHUNK
-X_BUFS = 4
-BIAS_BUFS = 5
+SBUF_TILES = {("x", 2): 2, ("x", 4): 2, ("bias", 2): 5}
 BIAS_AHEAD = 10
 LOADS = (
-    [("x", 2), ("bias", 1), ("x", 2), ("bias", 1)]
-    + [("bias", 2), ("x", 2)] * 5
-    + [("bias", 2), ("bias", 2)]
+    [("x", 2)]
+    + [("x", 2), ("bias", 2)] * 3
+    + [("x", 4), ("bias", 2), ("bias", 2)] * 2
+    + [("bias", 2)]
 )
 
 FLOPS = 2 * ROWS * RANKS * K_RANK * COLS
@@ -44,8 +44,7 @@ def tile_gemmrstritonpcie_t_e_kernel(tc, x, weight_words, weight_scales, bias, o
     with ExitStack() as ctx:
         ctx.enter_context(tc.manual_schedule())
         keep = ctx.enter_context(tc.tile_pool(name="keep", bufs=1))
-        x_pool = ctx.enter_context(tc.tile_pool(name="x", bufs=X_BUFS))
-        bias_pool = ctx.enter_context(tc.tile_pool(name="bias", bufs=BIAS_BUFS))
+        load_pool = ctx.enter_context(tc.tile_pool(name="loads", bufs=2))
         stage = ctx.enter_context(tc.tile_pool(name="stage", bufs=2))
         ahead = ctx.enter_context(tc.tile_pool(name="ahead", bufs=3))
         mx_pool = ctx.enter_context(tc.tile_pool(name="mx", bufs=4))
@@ -89,13 +88,17 @@ def tile_gemmrstritonpcie_t_e_kernel(tc, x, weight_words, weight_scales, bias, o
             )
 
         def load_x(first, count):
-            rows = x_pool.tile([P, RANKS, count, K_RANK], BF16, name="x_tiles")
+            rows = load_pool.tile(
+                [P, RANKS, count, K_RANK], BF16, name="x_by_%d" % count, bufs=SBUF_TILES[("x", count)]
+            )
             nc.sync.dma_start(out=rows[:], in_=x_rows[:, :, first : first + count, :])
             for i in range(count):
                 x_tile[first + i] = rows[:, :, i, :]
 
         def load_bias(first, count):
-            rows = bias_pool.tile([P, RANKS, count, COLS], BF16, name="bias_tiles")
+            rows = load_pool.tile(
+                [P, RANKS, count, COLS], BF16, name="bias_by_%d" % count, bufs=SBUF_TILES[("bias", count)]
+            )
             nc.sync.dma_start(out=rows[:], in_=bias_rows[:, :, first : first + count, :])
             for i in range(count):
                 bias_tile[first + i] = rows[:, :, i, :]
@@ -221,26 +224,26 @@ def tile_gemmrstritonpcie_t_e_kernel(tc, x, weight_words, weight_scales, bias, o
 
         to_load = list(LOADS)
         next_tile = {"x": 0, "bias": 0}
-        issued = {"x": [], "bias": []}
+        issued = {size: [] for size in SBUF_TILES}
         done_with = {"x": set(), "bias": set()}
 
         def load_what_fits():
             while len(to_load) > 0:
-                what, count = to_load[0]
-                load, bufs = {"x": (load_x, X_BUFS), "bias": (load_bias, BIAS_BUFS)}[what]
-                if len(issued[what]) >= bufs and not issued[what][-bufs] <= done_with[what]:
+                size = to_load[0]
+                what, count = size
+                bufs = SBUF_TILES[size]
+                if len(issued[size]) >= bufs and not issued[size][-bufs] <= done_with[what]:
                     return
                 first = next_tile[what]
+                load = {"x": load_x, "bias": load_bias}[what]
                 load(first, count)
-                issued[what].append(set(range(first, first + count)))
+                issued[size].append(set(range(first, first + count)))
                 next_tile[what] = first + count
-                to_load.remove(to_load[0])
+                to_load.remove(size)
+                if what == "x" and first == 0:
+                    load_scales()
+                    load_weight()
 
-        load_x(0, CHUNK)
-        issued["x"].append(set(range(CHUNK)))
-        next_tile["x"] = CHUNK
-        load_scales()
-        load_weight()
         load_what_fits()
 
         to_store = []

from contextlib import ExitStack

import concourse.mybir as mybir
from concourse.masks import make_identity

BF16 = mybir.dt.bfloat16
F32 = mybir.dt.float32
I32 = mybir.dt.int32
U32 = mybir.dt.uint32
U8 = mybir.dt.uint8
FP8X4 = mybir.dt.float8_e4m3fn_x4
ADD = mybir.AluOpType.add

P = 128
RANKS = 4
ROWS = 2048
K_RANK = 512
COLS = 1024
HALF = 512
ROW_TILES = ROWS // P
CHUNK = 2
CHUNKS = ROW_TILES // CHUNK
SBUF_TILES = {("x", 2): 2, ("x", 4): 2, ("bias", 2): 5}
BIAS_AHEAD = 10
LOADS = (
    [("x", 2)]
    + [("x", 2), ("bias", 2)] * 3
    + [("x", 4), ("bias", 2), ("bias", 2)] * 2
    + [("bias", 2)]
)

FLOPS = 2 * ROWS * RANKS * K_RANK * COLS


def tile_gemmrstritonpcie_t_e_kernel(tc, x, weight_words, weight_scales, bias, out):
    nc = tc.nc
    left = slice(0, HALF)
    right = slice(HALF, COLS)

    x_rows = x.rearrange("r (p t) k -> p r t k", t=ROW_TILES)
    bias_rows = bias.rearrange("r (p t) n -> p r t n", t=ROW_TILES)
    out_rows = out.rearrange("w (q t) n -> (w q) t n", t=ROW_TILES)

    with ExitStack() as ctx:
        ctx.enter_context(tc.manual_schedule())
        keep = ctx.enter_context(tc.tile_pool(name="keep", bufs=1))
        load_pool = ctx.enter_context(tc.tile_pool(name="loads", bufs=2))
        stage = ctx.enter_context(tc.tile_pool(name="stage", bufs=2))
        ahead = ctx.enter_context(tc.tile_pool(name="ahead", bufs=3))
        mx_pool = ctx.enter_context(tc.tile_pool(name="mx", bufs=4))
        out_pool = ctx.enter_context(tc.tile_pool(name="out", bufs=6))
        flip_psum = ctx.enter_context(tc.psum_pool(name="flip", bufs=2))
        acc_psum = ctx.enter_context(tc.psum_pool(name="acc", bufs=2))

        x_tile = {}
        bias_tile = {}
        sorted_words = {}
        grouped = {}
        x_codes = {}
        x_scales = {}
        product = {}
        bias_sum = {}
        left_part = {}
        right_part = {}
        result = {}
        right_bias = {}

        ident_f32 = keep.tile([P, P], F32)
        make_identity(nc, ident_f32[:])
        ident_bf16 = keep.tile([P, P], BF16)
        make_identity(nc, ident_bf16[:])

        w_planes = keep.tile([P, COLS], U8, align_bytes=64)
        nc.vector.memset(w_planes[:].bitcast(I32), 0)
        w_words = keep.tile([P, RANKS, COLS], U32, align_bytes=64)

        def load_scales():
            for quadrant in range(4):
                nc.sync.dma_start(
                    out=w_planes[32 * quadrant : 32 * quadrant + 16, :].bitcast(I32),
                    in_=weight_scales[:, 4 * quadrant : 4 * quadrant + 4, :].bitcast(I32),
                )

        def load_weight():
            nc.sync.dma_start(
                out=w_words[:].bitcast(I32),
                in_=weight_words.rearrange("g p n t -> p g (n t)").bitcast(I32),
            )

        def load_x(first, count):
            rows = load_pool.tile(
                [P, RANKS, count, K_RANK], BF16, name="x_by_%d" % count, bufs=SBUF_TILES[("x", count)]
            )
            nc.sync.dma_start(out=rows[:], in_=x_rows[:, :, first : first + count, :])
            for i in range(count):
                x_tile[first + i] = rows[:, :, i, :]

        def load_bias(first, count):
            rows = load_pool.tile(
                [P, RANKS, count, COLS], BF16, name="bias_by_%d" % count, bufs=SBUF_TILES[("bias", count)]
            )
            nc.sync.dma_start(out=rows[:], in_=bias_rows[:, :, first : first + count, :])
            for i in range(count):
                bias_tile[first + i] = rows[:, :, i, :]

        def bias_block(r, t, cols):
            return bias_tile[t][:, r, cols]

        def sort_words(t):
            words = x_tile[t].bitcast(F32)
            sorted_words[t] = stage.tile([P, RANKS, 2, P], F32, name="sorted_words")
            nc.scalar.copy(out=sorted_words[t][:], in_=words.rearrange("p r (j u) -> p r u j", u=2))

        def flip(t):
            grouped[t] = stage.tile([P, RANKS, P, 4], BF16, name="grouped", align_bytes=64)
            grouped_words = (
                grouped[t][:]
                .rearrange("p r c f -> p (r c f)")
                .bitcast(F32)
                .rearrange("p (r c u) -> p r c u", r=RANKS, u=2)
            )
            for pair in range(RANKS // 2):
                flipped = flip_psum.tile([P, 2, 2, P], F32, name="flipped")
                for a in range(2):
                    for u in range(2):
                        nc.tensor.transpose(
                            flipped[:, a, u, :], sorted_words[t][:, 2 * pair + a, u, :], ident_f32[:]
                        )
                nc.scalar.copy(
                    out=grouped_words[:, 2 * pair : 2 * pair + 2, :, :],
                    in_=flipped[:].rearrange("p a u c -> p a c u"),
                )

        def quantise(t):
            x_codes[t] = mx_pool.tile([P, RANKS * P], U32, name="x_codes", align_bytes=64)
            x_scales[t] = mx_pool.tile([P, RANKS * P], U8, name="x_scales", align_bytes=64)
            nc.vector.quantize_mx(
                out=x_codes[t][:].bitcast(FP8X4),
                scales=x_scales[t][:],
                in_=grouped[t][:].rearrange("p r c f -> p (r c f)"),
            )

        def multiply(t):
            product[(t, 0)] = acc_psum.tile([P, HALF], F32, name="product_left")
            product[(t, 1)] = acc_psum.tile([P, HALF], F32, name="product_right")
            for g in range(RANKS):
                rows = slice(g * P, (g + 1) * P)
                for h, cols in enumerate((left, right)):
                    nc.tensor.matmul_mx(
                        out=product[(t, h)][:],
                        lhsT=x_codes[t][:, rows].bitcast(FP8X4),
                        lhsT_scale=x_scales[t][:, rows],
                        rhs=w_words[:, g, cols].bitcast(FP8X4),
                        rhs_scale=w_planes[4 * g : P, cols],
                        start=(g == 0),
                        stop=(g == RANKS - 1),
                    )

        def sum_bias_on_tensor(t):
            bias_sum[t] = acc_psum.tile([P, HALF], F32, name="bias_sum")
            for r in range(1, RANKS):
                nc.tensor.matmul(
                    out=bias_sum[t][:],
                    lhsT=ident_bf16[:],
                    rhs=bias_block(r, t, left),
                    start=(r == 1),
                    stop=(r == RANKS - 1),
                )

        def take_products(t):
            left_part[t] = stage.tile([P, HALF], F32, name="left_part")
            right_part[t] = stage.tile([P, HALF], F32, name="right_part")
            nc.vector.tensor_tensor(
                out=right_part[t][:], in0=product[(t, 1)][:], in1=bias_block(0, t, right), op=ADD
            )
            nc.vector.tensor_tensor(
                out=left_part[t][:], in0=product[(t, 0)][:], in1=bias_block(0, t, left), op=ADD
            )

        def sum_bias_on_gpsimd(t):
            right_bias[t] = ahead.tile([P, HALF], F32, name="right_bias")
            nc.gpsimd.tensor_tensor(
                out=right_bias[t][:], in0=bias_block(1, t, right), in1=bias_block(2, t, right), op=ADD
            )
            nc.gpsimd.tensor_tensor(
                out=right_bias[t][:], in0=right_bias[t][:], in1=bias_block(3, t, right), op=ADD
            )

        def result_rows(t):
            if t % CHUNK == 0:
                result[t // CHUNK] = out_pool.tile([P, CHUNK, COLS], F32, name="result")
            return result[t // CHUNK][:, t % CHUNK, :]

        def finish(t):
            rows = result_rows(t)
            nc.vector.tensor_tensor(
                out=rows[:, right], in0=right_part[t][:], in1=right_bias[t][:], op=ADD
            )
            nc.vector.tensor_tensor(
                out=rows[:, left], in0=bias_sum[t][:], in1=left_part[t][:], op=ADD
            )

        def store(t):
            if t // CHUNK == CHUNKS - 1:
                nc.sync.dma_start(out=out_rows[:, t, :], in_=result[t // CHUNK][:, t % CHUNK, :])
            elif t % CHUNK == CHUNK - 1:
                nc.sync.dma_start(
                    out=out_rows[:, t - CHUNK + 1 : t + 1, :], in_=result[t // CHUNK][:]
                )

        def finish_and_store_last(t):
            rows = result_rows(t)
            nc.vector.tensor_tensor(
                out=rows[:, right], in0=right_part[t][:], in1=right_bias[t][:], op=ADD
            )
            nc.sync.dma_start(out=out_rows[:, t, right], in_=rows[:, right])
            nc.vector.tensor_tensor(
                out=rows[:, left], in0=bias_sum[t][:], in1=left_part[t][:], op=ADD
            )
            nc.sync.dma_start(out=out_rows[:, t, left], in_=rows[:, left])

        def is_tile(t):
            return 0 <= t < ROW_TILES

        to_load = list(LOADS)
        next_tile = {"x": 0, "bias": 0}
        issued = {size: [] for size in SBUF_TILES}
        done_with = {"x": set(), "bias": set()}

        def load_what_fits():
            while len(to_load) > 0:
                size = to_load[0]
                what, count = size
                bufs = SBUF_TILES[size]
                if len(issued[size]) >= bufs and not issued[size][-bufs] <= done_with[what]:
                    return
                first = next_tile[what]
                load = {"x": load_x, "bias": load_bias}[what]
                load(first, count)
                issued[size].append(set(range(first, first + count)))
                next_tile[what] = first + count
                to_load.remove(size)
                if what == "x" and first == 0:
                    load_scales()
                    load_weight()

        load_what_fits()

        to_store = []

        def finish_and_store(t):
            if t == ROW_TILES - 1:
                finish_and_store_last(t)
            else:
                finish(t)
                to_store.append(t)

        for t in range(-4, ROW_TILES):
            bias_first = t >= BIAS_AHEAD
            if is_tile(t):
                take_products(t)
            if is_tile(t + 2):
                quantise(t + 2)
            if is_tile(t - 1) and t <= BIAS_AHEAD:
                finish_and_store(t - 1)
            if bias_first:
                sum_bias_on_tensor(t)
            if is_tile(t + 1):
                multiply(t + 1)
            if is_tile(t + 3):
                flip(t + 3)
            if is_tile(t + 4):
                sort_words(t + 4)
                done_with["x"].add(t + 4)
                load_what_fits()
            if is_tile(t):
                if not bias_first:
                    sum_bias_on_tensor(t)
                sum_bias_on_gpsimd(t)
                if bias_first:
                    finish_and_store(t)
                done_with["bias"].add(t)
                load_what_fits()
            if len(to_load) == 0:
                for finished in to_store:
                    store(finished)
                to_store.clear()
